import numpy as np
import ml_dtypes


def mxq(x, axis, fmt="e4m3"):
    dtype, down = {"e4m3": (ml_dtypes.float8_e4m3fn, 7), "e5m2": (ml_dtypes.float8_e5m2, 14)}[fmt]
    v = np.moveaxis(np.asarray(x, np.float32).astype(ml_dtypes.bfloat16).astype(np.float64), axis, -1)
    blocks = v.reshape(v.shape[:-1] + (-1, 32))
    amax = np.abs(blocks).max(-1, keepdims=True)
    byte = np.maximum(np.where(amax > 0, np.frexp(amax)[1] - 1 + 127, 0) - down, 1)
    scale = np.exp2(byte - 127.0)
    codes = (blocks / scale).astype(np.float32).astype(dtype).astype(np.float64)
    return np.moveaxis((codes * scale).reshape(v.shape), -1, axis)


WIDE = False


def mx_kscale(k):
    if not WIDE:
        return np.ones(k)
    levels = np.array([10, -10, 5, -5, 0])
    a = np.random.permutation(np.resize(levels, k // 512 * 4)).reshape(k // 512, 4)
    idx = np.arange(k)
    return np.exp2(a[idx // 512, idx % 128 // 32])


BF16 = ml_dtypes.bfloat16


def bf(x):
    return np.asarray(x, np.float32).astype(BF16)


def f64(x):
    return np.asarray(x).astype(np.float64)


E2M1 = np.array([0.0, 0.5, 1.0, 1.5, 2.0, 3.0, 4.0, 6.0, -0.0, -0.5, -1.0, -1.5, -2.0, -3.0, -4.0, -6.0])


def pack_weight(w, fmt):
    k, n = w.shape
    w = f64(bf(w)).reshape(k // 32, 32, n)
    amax = np.abs(w).max(1)
    if fmt == "e4m3":
        byte = np.frexp(amax)[1] - 1 + 127 - 7
    else:
        mant, ex = np.frexp(amax / 6.0)
        byte = np.where(mant > 0.5, ex, ex - 1) + 127
    byte = np.clip(np.where(amax > 0, byte, 1), 1, 254)
    scaled = (w * np.exp2(127.0 - byte)[:, None, :]).reshape(k, n).astype(np.float32)
    by_word = np.ascontiguousarray(scaled.reshape(k // 512, 128, 4, n).transpose(0, 1, 3, 2))
    if fmt == "e4m3":
        words = by_word.astype(ml_dtypes.float8_e4m3fn).view(np.uint8)
    else:
        c = by_word.astype(ml_dtypes.float4_e2m1fn).view(np.uint8) & 0xF
        words = c[..., 0::2] | (c[..., 1::2] << 4)
    return np.ascontiguousarray(words), np.ascontiguousarray(byte.astype(np.uint8).reshape(k // 512, 16, n))


def unpack_weight(words, scales, fmt):
    g, p, n, _ = words.shape
    if fmt == "e4m3":
        vals = np.ascontiguousarray(words).view(ml_dtypes.float8_e4m3fn).astype(np.float64)
    else:
        nib = np.empty((g, p, n, 4), np.uint8)
        nib[..., 0::2] = words & 0xF
        nib[..., 1::2] = words >> 4
        vals = E2M1[nib]
    vals = vals * np.repeat(np.exp2(scales.astype(np.float64) - 127.0), 8, axis=1)[..., None]
    return vals.transpose(0, 1, 3, 2).reshape(g * 512, n)


B, T, D, E, F = 4, 32, 8192, 1024, 2048
EPS = 1e-6
FMT = "e4m3"


def rms_norm(x, w):
    rms = np.sqrt(np.mean(x * x, axis=-1, keepdims=True) + EPS)
    return x / rms * w


def erf(v):
    a = np.minimum(np.abs(v), 6.0)
    z = 2.0 * a * a
    term = a.copy()
    tot = a.copy()
    for n in range(1, 110):
        term = term * z / (2 * n + 1)
        tot = tot + term
    return np.sign(v) * tot * np.exp(-a * a) * 2.0 / np.sqrt(np.pi)


def gelu_erf(v):
    return 0.5 * v * (1.0 + erf(v / np.sqrt(2.0)))


def setup_inputs():
    s, t = mx_kscale(E), mx_kscale(D)
    attn = bf(np.random.standard_normal((B, T, E)) * 0.6 * s)
    x = bf(np.random.standard_normal((B, T, D)))
    wo_words, wo_scales = pack_weight(np.random.standard_normal((E, D)) / np.sqrt(E) / s[:, None], FMT)
    bo = bf(np.random.standard_normal(D) * 0.1)
    mlp_norm_w = bf((1.0 + 0.1 * np.random.standard_normal(D)) * t)
    w1_words, w1_scales = pack_weight(np.random.standard_normal((D, F)) / np.sqrt(D) / t[:, None], FMT)
    b1 = bf(np.random.standard_normal(F) * 0.1)
    return {"attn": attn,
            "x": x,
            "wo_words": wo_words,
            "wo_scales": wo_scales,
            "bo": bo,
            "mlp_norm_w": mlp_norm_w,
            "w1_words": w1_words,
            "w1_scales": w1_scales,
            "b1": b1}


def reference(attn, x, wo_words, wo_scales, bo, mlp_norm_w, w1_words, w1_scales, b1):
    x_mid = f64(x) + (mxq(f64(attn), 2, "e4m3") @ unpack_weight(wo_words, wo_scales, FMT)) + f64(bo)
    h = rms_norm(x_mid, f64(mlp_norm_w))
    g = gelu_erf((mxq(h, 2, "e4m3") @ unpack_weight(w1_words, w1_scales, FMT)) + f64(b1))
    return x_mid, g

@@ -1,0 +1,271 @@
+from contextlib import ExitStack
+
+import concourse.mybir as mybir
+from concourse.masks import make_identity
+
+F32 = mybir.dt.float32
+BF16 = mybir.dt.bfloat16
+I32 = mybir.dt.int32
+U32 = mybir.dt.uint32
+U8 = mybir.dt.uint8
+FP8X4 = mybir.dt.float8_e4m3fn_x4
+ADD = mybir.AluOpType.add
+MULT = mybir.AluOpType.mult
+ACT = mybir.ActivationFunctionType
+
+P = 128
+E = 1024
+D = 8192
+F = 2048
+EPS = 1e-6
+K_PASS = 512
+BANK = 512
+QUARTER = 2048
+E_PASSES = E // K_PASS
+D_PASSES = D // K_PASS
+QUARTERS = D // QUARTER
+BANKS_PER_QUARTER = QUARTER // BANK
+PASSES_PER_QUARTER = QUARTER // K_PASS
+F_BANKS = F // BANK
+PLANES = 4
+QUADRANT = 32
+
+BO_ROW = 0
+GAIN_ROW = D // BANK
+B1_ROW = 2 * (D // BANK)
+
+WEIGHT_BUFS = 12
+HELD_BACK = 1
+
+FLOPS = 2 * P * E * D + 2 * P * D * F
+
+
+def tile_tinyblock_pb_k_kernel(
+    tc, attn, x, wo_words, wo_scales, bo, mlp_norm_w, w1_words, w1_scales, b1, out_0, out_1
+):
+    nc = tc.nc
+    x_mid_out = out_0.flatten_outer_dims()
+    g_out = out_1.flatten_outer_dims()
+
+    with ExitStack() as ctx:
+        ctx.enter_context(tc.manual_schedule())
+        const = ctx.enter_context(tc.tile_pool(name="const", bufs=1))
+        weights = ctx.enter_context(tc.tile_pool(name="weights", bufs=WEIGHT_BUFS))
+        stage = ctx.enter_context(tc.tile_pool(name="stage", bufs=2))
+        work = ctx.enter_context(tc.psum_pool(name="work", bufs=4))
+        out_acc = ctx.enter_context(tc.psum_pool(name="out_acc", bufs=1))
+
+        eps_col = const.tile([P, 1], F32)
+        nc.vector.memset(eps_col[:], EPS)
+        vec_rows = const.tile([P, BANK], BF16)
+        nc.vector.memset(vec_rows[:], 0.0)
+        wo_planes = const.tile([P, E_PASSES * QUARTER], U8, align_bytes=64)
+        nc.vector.memset(wo_planes[:].bitcast(I32), 0)
+        w1_planes = const.tile([P, (D_PASSES // PLANES) * F], U8, align_bytes=64)
+        nc.vector.memset(w1_planes[:].bitcast(I32), 0)
+        warm = const.tile([P, 1], F32)
+        nc.scalar.activation(out=warm[:], in_=eps_col[:], func=ACT.Sqrt)
+        ident_f32 = const.tile([P, P], F32)
+        make_identity(nc, ident_f32[:])
+        ident_bf16 = const.tile([P, P], BF16)
+        make_identity(nc, ident_bf16[:])
+
+        attn_sb = const.tile([P, E], BF16)
+        nc.sync.dma_start(out=attn_sb[:], in_=attn.flatten_outer_dims())
+        x_sb = const.tile([P, D], BF16)
+        nc.sync.dma_start(out=x_sb[:], in_=x.flatten_outer_dims())
+        nc.sync.dma_start(out=vec_rows[BO_ROW : BO_ROW + D // BANK, :], in_=bo.rearrange("(r n) -> r n", n=BANK))
+        nc.sync.dma_start(
+            out=vec_rows[GAIN_ROW : GAIN_ROW + D // BANK, :], in_=mlp_norm_w.rearrange("(r n) -> r n", n=BANK)
+        )
+        nc.sync.dma_start(out=vec_rows[B1_ROW : B1_ROW + F // BANK, :], in_=b1.rearrange("(r n) -> r n", n=BANK))
+
+        for g in range(E_PASSES):
+            for quad in range(P // QUADRANT):
+                nc.sync.dma_start(
+                    out=wo_planes[
+                        QUADRANT * quad : QUADRANT * quad + 4 * PLANES, g * QUARTER : (g + 1) * QUARTER
+                    ].bitcast(I32),
+                    in_=wo_scales[g, 4 * quad : 4 * quad + 4, :].bitcast(I32).rearrange("r (b n) -> b r n", b=PLANES),
+                )
+        for a in range(D_PASSES // PLANES):
+            for quad in range(P // QUADRANT):
+                nc.sync.dma_start(
+                    out=w1_planes[QUADRANT * quad : QUADRANT * quad + 4 * PLANES, a * F : (a + 1) * F].bitcast(I32),
+                    in_=w1_scales[PLANES * a : PLANES * (a + 1), 4 * quad : 4 * quad + 4, :].bitcast(I32),
+                )
+
+        def load_words(words, name):
+            tile_of_words = weights.tile([P, QUARTER], U32, name=name, tag="weights", align_bytes=64)
+            nc.sync.dma_start(out=tile_of_words[:].bitcast(I32), in_=words.bitcast(I32))
+            return tile_of_words
+
+        wo_tiles = {}
+        for q in range(QUARTERS):
+            for g in range(E_PASSES):
+                all_columns = wo_words[g].rearrange("p n t -> p (n t)")
+                wo_tiles[(g, q)] = load_words(all_columns[:, 4 * QUARTER * q : 4 * QUARTER * (q + 1)], "wo_words_sb")
+
+        w1_tiles = []
+
+        def load_w1(count):
+            for g in range(len(w1_tiles), len(w1_tiles) + count):
+                w1_tiles.append(load_words(w1_words[g].rearrange("p n t -> p (n t)"), "w1_words_sb"))
+
+        load_w1(WEIGHT_BUFS - len(wo_tiles))
+
+        attn_words = attn_sb[:].bitcast(F32)
+        attn_t = work.tile([P, E_PASSES, 2, P], F32, tag="bank")
+        for g in range(E_PASSES):
+            for u in range(2):
+                nc.tensor.transpose(
+                    attn_t[:, g, u, :], attn_words[:, 256 * g + u : 256 * (g + 1) : 2], ident_f32[:]
+                )
+        attn_grouped = const.tile([P, 4 * E_PASSES * P], BF16, align_bytes=64)
+        nc.vector.tensor_copy(
+            out=attn_grouped[:].bitcast(F32).rearrange("p (g r u) -> p g r u", g=E_PASSES, u=2),
+            in_=attn_t[:].rearrange("p g u r -> p g r u"),
+        )
+        attn_codes = const.tile([P, E_PASSES * P], U32, align_bytes=64)
+        attn_scales = const.tile([P, E_PASSES * P], U8, align_bytes=64)
+        nc.vector.quantize_mx(out=attn_codes[:].bitcast(FP8X4), scales=attn_scales[:], in_=attn_grouped[:])
+
+        def spread_row(row, name):
+            bank = work.tile([P, BANK], F32, name=name, tag="bank")
+            nc.tensor.matmul(
+                out=bank[:],
+                lhsT=ident_bf16[:, row : row + 1].to_broadcast([P, P]),
+                rhs=vec_rows[:],
+                start=True,
+                stop=True,
+            )
+            return bank
+
+        x_mid = [const.tile([P, QUARTER], F32, name="x_mid_%d" % q) for q in range(QUARTERS)]
+        gain_rows = const.tile([P, D], BF16)
+        b1_rows = const.tile([P, F], BF16)
+        for c in range(D // BANK):
+            q, j = divmod(c, BANKS_PER_QUARTER)
+            bo_bank = spread_row(BO_ROW + c, "bo_bank")
+            nc.vector.tensor_tensor(
+                out=x_mid[q][:, j * BANK : (j + 1) * BANK],
+                in0=bo_bank[:],
+                in1=x_sb[:, c * BANK : (c + 1) * BANK],
+                op=ADD,
+            )
+            gain_bank = spread_row(GAIN_ROW + c, "gain_bank")
+            nc.scalar.copy(out=gain_rows[:, c * BANK : (c + 1) * BANK], in_=gain_bank[:])
+        for n in range(F_BANKS):
+            b1_bank = spread_row(B1_ROW + n, "b1_bank")
+            nc.scalar.copy(out=b1_rows[:, n * BANK : (n + 1) * BANK], in_=b1_bank[:])
+
+        sum_sq = const.tile([P, D // BANK], F32)
+        for q in range(QUARTERS):
+            for j in range(BANKS_PER_QUARTER):
+                columns = slice(j * BANK, (j + 1) * BANK)
+                acc = work.tile([P, BANK], F32, tag="bank")
+                for g in range(E_PASSES):
+                    nc.tensor.matmul_mx(
+                        out=acc[:],
+                        lhsT=attn_codes[:, g * P : (g + 1) * P].bitcast(FP8X4),
+                        lhsT_scale=attn_scales[:, g * P : (g + 1) * P],
+                        rhs=wo_tiles[(g, q)][:, columns].bitcast(FP8X4),
+                        rhs_scale=wo_planes[4 * q : P, g * QUARTER + j * BANK : g * QUARTER + (j + 1) * BANK],
+                        start=(g == 0),
+                        stop=(g == E_PASSES - 1),
+                    )
+                nc.vector.tensor_tensor(out=x_mid[q][:, columns], in0=acc[:], in1=x_mid[q][:, columns], op=ADD)
+                squares = stage.tile([P, BANK], BF16)
+                c = q * BANKS_PER_QUARTER + j
+                nc.scalar.activation(
+                    out=squares[:], in_=x_mid[q][:, columns], func=ACT.Square, accum_out=sum_sq[:, c : c + 1]
+                )
+            if q < QUARTERS - HELD_BACK:
+                nc.scalar.dma_start(out=x_mid_out[:, q * QUARTER : (q + 1) * QUARTER], in_=x_mid[q][:])
+            load_w1(E_PASSES)
+
+        total_sq = const.tile([P, 1], F32)
+        nc.vector.reduce_sum(out=total_sq[:], in_=sum_sq[:], axis=mybir.AxisListType.X)
+        rms = const.tile([P, 1], F32)
+        nc.scalar.activation(out=rms[:], in_=total_sq[:], func=ACT.Sqrt, scale=1.0 / D, bias=eps_col[:])
+        inv_rms = const.tile([P, 1], F32)
+        nc.vector.reciprocal(out=inv_rms[:], in_=rms[:])
+        nc.scalar.activation(out=warm[:], in_=rms[:], func=ACT.Gelu)
+
+        h_codes = const.tile([P, D_PASSES * P], U32, align_bytes=64)
+        h_scales = const.tile([P, D_PASSES * P], U8, align_bytes=64)
+        h_sorted = {}
+        h_grouped = {}
+
+        def scale_rows(q):
+            h_sorted[q] = stage.tile([P, QUARTER], BF16, name="h_sorted")
+            for u in range(2):
+                nc.vector.scalar_tensor_tensor(
+                    out=h_sorted[q][:, u * (QUARTER // 2) : (u + 1) * (QUARTER // 2)].rearrange(
+                        "r (i e) -> r i e", e=2
+                    ),
+                    in0=x_mid[q][:].rearrange("r (i u e) -> r u i e", u=2, e=2)[:, u],
+                    scalar=inv_rms[:],
+                    in1=gain_rows[:, q * QUARTER : (q + 1) * QUARTER].rearrange("r (i u e) -> r u i e", u=2, e=2)[:, u],
+                    op0=MULT,
+                    op1=MULT,
+                )
+
+        def transpose_rows(q):
+            h_words = h_sorted[q][:].bitcast(F32)
+            h_grouped[q] = stage.tile([P, QUARTER], BF16, name="h_grouped", align_bytes=64)
+            grouped_words = h_grouped[q][:].bitcast(F32).rearrange("p (g r u) -> p g r u", g=PASSES_PER_QUARTER, u=2)
+            for half in range(2):
+                h_t = work.tile([P, 2, 2, P], F32, tag="bank")
+                for g in range(2):
+                    for u in range(2):
+                        first = u * (QUARTER // 4) + (2 * half + g) * P
+                        nc.tensor.transpose(h_t[:, g, u, :], h_words[:, first : first + P], ident_f32[:])
+                nc.scalar.copy(
+                    out=grouped_words[:, 2 * half : 2 * half + 2], in_=h_t[:].rearrange("p g u r -> p g r u")
+                )
+
+        def quantise_rows(q):
+            nc.vector.quantize_mx(
+                out=h_codes[:, q * K_PASS : (q + 1) * K_PASS].bitcast(FP8X4),
+                scales=h_scales[:, q * K_PASS : (q + 1) * K_PASS],
+                in_=h_grouped[q][:],
+            )
+
+        g_acc = [out_acc.tile([P, BANK], F32, name="g_acc_%d" % n) for n in range(F_BANKS)]
+
+        def multiply(q):
+            for b in range(PASSES_PER_QUARTER):
+                g = q * PASSES_PER_QUARTER + b
+                for n in range(F_BANKS):
+                    nc.tensor.matmul_mx(
+                        out=g_acc[n][:],
+                        lhsT=h_codes[:, g * P : (g + 1) * P].bitcast(FP8X4),
+                        lhsT_scale=h_scales[:, g * P : (g + 1) * P],
+                        rhs=w1_tiles[g][:, n * BANK : (n + 1) * BANK].bitcast(FP8X4),
+                        rhs_scale=w1_planes[4 * b : P, q * F + n * BANK : q * F + (n + 1) * BANK],
+                        start=(g == 0),
+                        stop=(g == D_PASSES - 1),
+                    )
+
+        scale_rows(0)
+        transpose_rows(0)
+        for q in range(QUARTERS):
+            if q + 1 < QUARTERS:
+                scale_rows(q + 1)
+            quantise_rows(q)
+            if q + 1 < QUARTERS:
+                transpose_rows(q + 1)
+            multiply(q)
+            if q == 0:
+                load_w1(D_PASSES - len(w1_tiles))
+                for held in range(QUARTERS - HELD_BACK, QUARTERS):
+                    nc.sync.dma_start(out=x_mid_out[:, held * QUARTER : (held + 1) * QUARTER], in_=x_mid[held][:])
+
+        for n in range(F_BANKS):
+            columns = slice(n * BANK, (n + 1) * BANK)
+            biased = stage.tile([P, BANK], F32)
+            nc.vector.tensor_tensor(out=biased[:], in0=g_acc[n][:], in1=b1_rows[:, columns], op=ADD)
+            g_sb = stage.tile([P, BANK], F32)
+            nc.scalar.activation(out=g_sb[:], in_=biased[:], func=ACT.Gelu)
+            nc.sync.dma_start(out=g_out[:, columns], in_=g_sb[:])

@@ -82,17 +82,17 @@ def tile_tinyblock_pb_k_kernel(
 
         for g in range(E_PASSES):
             for quad in range(P // QUADRANT):
-                nc.sync.dma_start(
+                nc.gpsimd.dma_start(
                     out=wo_planes[
                         QUADRANT * quad : QUADRANT * quad + 4 * PLANES, g * QUARTER : (g + 1) * QUARTER
-                    ].bitcast(I32),
-                    in_=wo_scales[g, 4 * quad : 4 * quad + 4, :].bitcast(I32).rearrange("r (b n) -> b r n", b=PLANES),
+                    ].bitcast(F32),
+                    in_=wo_scales[g, 4 * quad : 4 * quad + 4, :].bitcast(F32).rearrange("r (b n) -> b r n", b=PLANES),
                 )
         for a in range(D_PASSES // PLANES):
             for quad in range(P // QUADRANT):
-                nc.sync.dma_start(
-                    out=w1_planes[QUADRANT * quad : QUADRANT * quad + 4 * PLANES, a * F : (a + 1) * F].bitcast(I32),
-                    in_=w1_scales[PLANES * a : PLANES * (a + 1), 4 * quad : 4 * quad + 4, :].bitcast(I32),
+                nc.gpsimd.dma_start(
+                    out=w1_planes[QUADRANT * quad : QUADRANT * quad + 4 * PLANES, a * F : (a + 1) * F].bitcast(F32),
+                    in_=w1_scales[PLANES * a : PLANES * (a + 1), 4 * quad : 4 * quad + 4, :].bitcast(F32),
                 )
 
         def load_words(words, name):

@@ -35,7 +35,7 @@ GAIN_ROW = D // BANK
 B1_ROW = 2 * (D // BANK)
 
 WEIGHT_BUFS = 12
-HELD_BACK = 1
+HELD_BACK = 2
 
 FLOPS = 2 * P * E * D + 2 * P * D * F
 
@@ -62,7 +62,6 @@ def tile_tinyblock_pb_k_kernel(
         wo_planes = const.tile([P, E_PASSES * QUARTER], U8, align_bytes=64)
         nc.vector.memset(wo_planes[:].bitcast(I32), 0)
         w1_planes = const.tile([P, (D_PASSES // PLANES) * F], U8, align_bytes=64)
-        nc.vector.memset(w1_planes[:].bitcast(I32), 0)
         warm = const.tile([P, 1], F32)
         nc.scalar.activation(out=warm[:], in_=eps_col[:], func=ACT.Sqrt)
         ident_f32 = const.tile([P, P], F32)
@@ -88,11 +87,13 @@ def tile_tinyblock_pb_k_kernel(
                     ].bitcast(F32),
                     in_=wo_scales[g, 4 * quad : 4 * quad + 4, :].bitcast(F32).rearrange("r (b n) -> b r n", b=PLANES),
                 )
-        for a in range(D_PASSES // PLANES):
+
+        def fetch_w1_planes(q):
+            nc.vector.memset(w1_planes[:, q * F : (q + 1) * F].bitcast(I32), 0)
             for quad in range(P // QUADRANT):
                 nc.gpsimd.dma_start(
-                    out=w1_planes[QUADRANT * quad : QUADRANT * quad + 4 * PLANES, a * F : (a + 1) * F].bitcast(F32),
-                    in_=w1_scales[PLANES * a : PLANES * (a + 1), 4 * quad : 4 * quad + 4, :].bitcast(F32),
+                    out=w1_planes[QUADRANT * quad : QUADRANT * quad + 4 * PLANES, q * F : (q + 1) * F].bitcast(F32),
+                    in_=w1_scales[PLANES * q : PLANES * (q + 1), 4 * quad : 4 * quad + 4, :].bitcast(F32),
                 )
 
         def load_words(words, name):
@@ -182,6 +183,7 @@ def tile_tinyblock_pb_k_kernel(
                 )
             if q < QUARTERS - HELD_BACK:
                 nc.scalar.dma_start(out=x_mid_out[:, q * QUARTER : (q + 1) * QUARTER], in_=x_mid[q][:])
+            fetch_w1_planes(q)
             load_w1(E_PASSES)
 
         total_sq = const.tile([P, 1], F32)

@@ -34,7 +34,7 @@ BO_ROW = 0
 GAIN_ROW = D // BANK
 B1_ROW = 2 * (D // BANK)
 
-WEIGHT_BUFS = 12
+WEIGHT_BUFS = 14
 HELD_BACK = 2
 
 FLOPS = 2 * P * E * D + 2 * P * D * F

from contextlib import ExitStack

import concourse.mybir as mybir
from concourse.masks import make_identity

F32 = mybir.dt.float32
BF16 = mybir.dt.bfloat16
I32 = mybir.dt.int32
U32 = mybir.dt.uint32
U8 = mybir.dt.uint8
FP8X4 = mybir.dt.float8_e4m3fn_x4
ADD = mybir.AluOpType.add
MULT = mybir.AluOpType.mult
ACT = mybir.ActivationFunctionType

P = 128
E = 1024
D = 8192
F = 2048
EPS = 1e-6
K_PASS = 512
BANK = 512
QUARTER = 2048
E_PASSES = E // K_PASS
D_PASSES = D // K_PASS
QUARTERS = D // QUARTER
BANKS_PER_QUARTER = QUARTER // BANK
PASSES_PER_QUARTER = QUARTER // K_PASS
F_BANKS = F // BANK
PLANES = 4
QUADRANT = 32

BO_ROW = 0
GAIN_ROW = D // BANK
B1_ROW = 2 * (D // BANK)

WEIGHT_BUFS = 14
HELD_BACK = 2

FLOPS = 2 * P * E * D + 2 * P * D * F


def tile_tinyblock_pb_k_kernel(
    tc, attn, x, wo_words, wo_scales, bo, mlp_norm_w, w1_words, w1_scales, b1, out_0, out_1
):
    nc = tc.nc
    x_mid_out = out_0.flatten_outer_dims()
    g_out = out_1.flatten_outer_dims()

    with ExitStack() as ctx:
        ctx.enter_context(tc.manual_schedule())
        const = ctx.enter_context(tc.tile_pool(name="const", bufs=1))
        weights = ctx.enter_context(tc.tile_pool(name="weights", bufs=WEIGHT_BUFS))
        stage = ctx.enter_context(tc.tile_pool(name="stage", bufs=2))
        work = ctx.enter_context(tc.psum_pool(name="work", bufs=4))
        out_acc = ctx.enter_context(tc.psum_pool(name="out_acc", bufs=1))

        eps_col = const.tile([P, 1], F32)
        nc.vector.memset(eps_col[:], EPS)
        vec_rows = const.tile([P, BANK], BF16)
        nc.vector.memset(vec_rows[:], 0.0)
        wo_planes = const.tile([P, E_PASSES * QUARTER], U8, align_bytes=64)
        nc.vector.memset(wo_planes[:].bitcast(I32), 0)
        w1_planes = const.tile([P, (D_PASSES // PLANES) * F], U8, align_bytes=64)
        warm = const.tile([P, 1], F32)
        nc.scalar.activation(out=warm[:], in_=eps_col[:], func=ACT.Sqrt)
        ident_f32 = const.tile([P, P], F32)
        make_identity(nc, ident_f32[:])
        ident_bf16 = const.tile([P, P], BF16)
        make_identity(nc, ident_bf16[:])

        attn_sb = const.tile([P, E], BF16)
        nc.sync.dma_start(out=attn_sb[:], in_=attn.flatten_outer_dims())
        x_sb = const.tile([P, D], BF16)
        nc.sync.dma_start(out=x_sb[:], in_=x.flatten_outer_dims())
        nc.sync.dma_start(out=vec_rows[BO_ROW : BO_ROW + D // BANK, :], in_=bo.rearrange("(r n) -> r n", n=BANK))
        nc.sync.dma_start(
            out=vec_rows[GAIN_ROW : GAIN_ROW + D // BANK, :], in_=mlp_norm_w.rearrange("(r n) -> r n", n=BANK)
        )
        nc.sync.dma_start(out=vec_rows[B1_ROW : B1_ROW + F // BANK, :], in_=b1.rearrange("(r n) -> r n", n=BANK))

        for g in range(E_PASSES):
            for quad in range(P // QUADRANT):
                nc.gpsimd.dma_start(
                    out=wo_planes[
                        QUADRANT * quad : QUADRANT * quad + 4 * PLANES, g * QUARTER : (g + 1) * QUARTER
                    ].bitcast(F32),
                    in_=wo_scales[g, 4 * quad : 4 * quad + 4, :].bitcast(F32).rearrange("r (b n) -> b r n", b=PLANES),
                )

        def fetch_w1_planes(q):
            nc.vector.memset(w1_planes[:, q * F : (q + 1) * F].bitcast(I32), 0)
            for quad in range(P // QUADRANT):
                nc.gpsimd.dma_start(
                    out=w1_planes[QUADRANT * quad : QUADRANT * quad + 4 * PLANES, q * F : (q + 1) * F].bitcast(F32),
                    in_=w1_scales[PLANES * q : PLANES * (q + 1), 4 * quad : 4 * quad + 4, :].bitcast(F32),
                )

        def load_words(words, name):
            tile_of_words = weights.tile([P, QUARTER], U32, name=name, tag="weights", align_bytes=64)
            nc.sync.dma_start(out=tile_of_words[:].bitcast(I32), in_=words.bitcast(I32))
            return tile_of_words

        wo_tiles = {}
        for q in range(QUARTERS):
            for g in range(E_PASSES):
                all_columns = wo_words[g].rearrange("p n t -> p (n t)")
                wo_tiles[(g, q)] = load_words(all_columns[:, 4 * QUARTER * q : 4 * QUARTER * (q + 1)], "wo_words_sb")

        w1_tiles = []

        def load_w1(count):
            for g in range(len(w1_tiles), len(w1_tiles) + count):
                w1_tiles.append(load_words(w1_words[g].rearrange("p n t -> p (n t)"), "w1_words_sb"))

        load_w1(WEIGHT_BUFS - len(wo_tiles))

        attn_words = attn_sb[:].bitcast(F32)
        attn_t = work.tile([P, E_PASSES, 2, P], F32, tag="bank")
        for g in range(E_PASSES):
            for u in range(2):
                nc.tensor.transpose(
                    attn_t[:, g, u, :], attn_words[:, 256 * g + u : 256 * (g + 1) : 2], ident_f32[:]
                )
        attn_grouped = const.tile([P, 4 * E_PASSES * P], BF16, align_bytes=64)
        nc.vector.tensor_copy(
            out=attn_grouped[:].bitcast(F32).rearrange("p (g r u) -> p g r u", g=E_PASSES, u=2),
            in_=attn_t[:].rearrange("p g u r -> p g r u"),
        )
        attn_codes = const.tile([P, E_PASSES * P], U32, align_bytes=64)
        attn_scales = const.tile([P, E_PASSES * P], U8, align_bytes=64)
        nc.vector.quantize_mx(out=attn_codes[:].bitcast(FP8X4), scales=attn_scales[:], in_=attn_grouped[:])

        def spread_row(row, name):
            bank = work.tile([P, BANK], F32, name=name, tag="bank")
            nc.tensor.matmul(
                out=bank[:],
                lhsT=ident_bf16[:, row : row + 1].to_broadcast([P, P]),
                rhs=vec_rows[:],
                start=True,
                stop=True,
            )
            return bank

        x_mid = [const.tile([P, QUARTER], F32, name="x_mid_%d" % q) for q in range(QUARTERS)]
        gain_rows = const.tile([P, D], BF16)
        b1_rows = const.tile([P, F], BF16)
        for c in range(D // BANK):
            q, j = divmod(c, BANKS_PER_QUARTER)
            bo_bank = spread_row(BO_ROW + c, "bo_bank")
            nc.vector.tensor_tensor(
                out=x_mid[q][:, j * BANK : (j + 1) * BANK],
                in0=bo_bank[:],
                in1=x_sb[:, c * BANK : (c + 1) * BANK],
                op=ADD,
            )
            gain_bank = spread_row(GAIN_ROW + c, "gain_bank")
            nc.scalar.copy(out=gain_rows[:, c * BANK : (c + 1) * BANK], in_=gain_bank[:])
        for n in range(F_BANKS):
            b1_bank = spread_row(B1_ROW + n, "b1_bank")
            nc.scalar.copy(out=b1_rows[:, n * BANK : (n + 1) * BANK], in_=b1_bank[:])

        sum_sq = const.tile([P, D // BANK], F32)
        for q in range(QUARTERS):
            for j in range(BANKS_PER_QUARTER):
                columns = slice(j * BANK, (j + 1) * BANK)
                acc = work.tile([P, BANK], F32, tag="bank")
                for g in range(E_PASSES):
                    nc.tensor.matmul_mx(
                        out=acc[:],
                        lhsT=attn_codes[:, g * P : (g + 1) * P].bitcast(FP8X4),
                        lhsT_scale=attn_scales[:, g * P : (g + 1) * P],
                        rhs=wo_tiles[(g, q)][:, columns].bitcast(FP8X4),
                        rhs_scale=wo_planes[4 * q : P, g * QUARTER + j * BANK : g * QUARTER + (j + 1) * BANK],
                        start=(g == 0),
                        stop=(g == E_PASSES - 1),
                    )
                nc.vector.tensor_tensor(out=x_mid[q][:, columns], in0=acc[:], in1=x_mid[q][:, columns], op=ADD)
                squares = stage.tile([P, BANK], BF16)
                c = q * BANKS_PER_QUARTER + j
                nc.scalar.activation(
                    out=squares[:], in_=x_mid[q][:, columns], func=ACT.Square, accum_out=sum_sq[:, c : c + 1]
                )
            if q < QUARTERS - HELD_BACK:
                nc.scalar.dma_start(out=x_mid_out[:, q * QUARTER : (q + 1) * QUARTER], in_=x_mid[q][:])
            fetch_w1_planes(q)
            load_w1(E_PASSES)

        total_sq = const.tile([P, 1], F32)
        nc.vector.reduce_sum(out=total_sq[:], in_=sum_sq[:], axis=mybir.AxisListType.X)
        rms = const.tile([P, 1], F32)
        nc.scalar.activation(out=rms[:], in_=total_sq[:], func=ACT.Sqrt, scale=1.0 / D, bias=eps_col[:])
        inv_rms = const.tile([P, 1], F32)
        nc.vector.reciprocal(out=inv_rms[:], in_=rms[:])
        nc.scalar.activation(out=warm[:], in_=rms[:], func=ACT.Gelu)

        h_codes = const.tile([P, D_PASSES * P], U32, align_bytes=64)
        h_scales = const.tile([P, D_PASSES * P], U8, align_bytes=64)
        h_sorted = {}
        h_grouped = {}

        def scale_rows(q):
            h_sorted[q] = stage.tile([P, QUARTER], BF16, name="h_sorted")
            for u in range(2):
                nc.vector.scalar_tensor_tensor(
                    out=h_sorted[q][:, u * (QUARTER // 2) : (u + 1) * (QUARTER // 2)].rearrange(
                        "r (i e) -> r i e", e=2
                    ),
                    in0=x_mid[q][:].rearrange("r (i u e) -> r u i e", u=2, e=2)[:, u],
                    scalar=inv_rms[:],
                    in1=gain_rows[:, q * QUARTER : (q + 1) * QUARTER].rearrange("r (i u e) -> r u i e", u=2, e=2)[:, u],
                    op0=MULT,
                    op1=MULT,
                )

        def transpose_rows(q):
            h_words = h_sorted[q][:].bitcast(F32)
            h_grouped[q] = stage.tile([P, QUARTER], BF16, name="h_grouped", align_bytes=64)
            grouped_words = h_grouped[q][:].bitcast(F32).rearrange("p (g r u) -> p g r u", g=PASSES_PER_QUARTER, u=2)
            for half in range(2):
                h_t = work.tile([P, 2, 2, P], F32, tag="bank")
                for g in range(2):
                    for u in range(2):
                        first = u * (QUARTER // 4) + (2 * half + g) * P
                        nc.tensor.transpose(h_t[:, g, u, :], h_words[:, first : first + P], ident_f32[:])
                nc.scalar.copy(
                    out=grouped_words[:, 2 * half : 2 * half + 2], in_=h_t[:].rearrange("p g u r -> p g r u")
                )

        def quantise_rows(q):
            nc.vector.quantize_mx(
                out=h_codes[:, q * K_PASS : (q + 1) * K_PASS].bitcast(FP8X4),
                scales=h_scales[:, q * K_PASS : (q + 1) * K_PASS],
                in_=h_grouped[q][:],
            )

        g_acc = [out_acc.tile([P, BANK], F32, name="g_acc_%d" % n) for n in range(F_BANKS)]

        def multiply(q):
            for b in range(PASSES_PER_QUARTER):
                g = q * PASSES_PER_QUARTER + b
                for n in range(F_BANKS):
                    nc.tensor.matmul_mx(
                        out=g_acc[n][:],
                        lhsT=h_codes[:, g * P : (g + 1) * P].bitcast(FP8X4),
                        lhsT_scale=h_scales[:, g * P : (g + 1) * P],
                        rhs=w1_tiles[g][:, n * BANK : (n + 1) * BANK].bitcast(FP8X4),
                        rhs_scale=w1_planes[4 * b : P, q * F + n * BANK : q * F + (n + 1) * BANK],
                        start=(g == 0),
                        stop=(g == D_PASSES - 1),
                    )

        scale_rows(0)
        transpose_rows(0)
        for q in range(QUARTERS):
            if q + 1 < QUARTERS:
                scale_rows(q + 1)
            quantise_rows(q)
            if q + 1 < QUARTERS:
                transpose_rows(q + 1)
            multiply(q)
            if q == 0:
                load_w1(D_PASSES - len(w1_tiles))
                for held in range(QUARTERS - HELD_BACK, QUARTERS):
                    nc.sync.dma_start(out=x_mid_out[:, held * QUARTER : (held + 1) * QUARTER], in_=x_mid[held][:])

        for n in range(F_BANKS):
            columns = slice(n * BANK, (n + 1) * BANK)
            biased = stage.tile([P, BANK], F32)
            nc.vector.tensor_tensor(out=biased[:], in0=g_acc[n][:], in1=b1_rows[:, columns], op=ADD)
            g_sb = stage.tile([P, BANK], F32)
            nc.scalar.activation(out=g_sb[:], in_=biased[:], func=ACT.Gelu)
            nc.sync.dma_start(out=g_out[:, columns], in_=g_sb[:])
